import numpy as np
import ml_dtypes


def mxq(x, axis, fmt="e4m3"):
    dtype, down = {"e4m3": (ml_dtypes.float8_e4m3fn, 7), "e5m2": (ml_dtypes.float8_e5m2, 14)}[fmt]
    v = np.moveaxis(np.asarray(x, np.float32).astype(ml_dtypes.bfloat16).astype(np.float64), axis, -1)
    blocks = v.reshape(v.shape[:-1] + (-1, 32))
    amax = np.abs(blocks).max(-1, keepdims=True)
    byte = np.maximum(np.where(amax > 0, np.frexp(amax)[1] - 1 + 127, 0) - down, 1)
    scale = np.exp2(byte - 127.0)
    codes = (blocks / scale).astype(np.float32).astype(dtype).astype(np.float64)
    return np.moveaxis((codes * scale).reshape(v.shape), -1, axis)


WIDE = False


def mx_kscale(k):
    if not WIDE:
        return np.ones(k)
    levels = np.array([10, -10, 5, -5, 0])
    a = np.random.permutation(np.resize(levels, k // 512 * 4)).reshape(k // 512, 4)
    idx = np.arange(k)
    return np.exp2(a[idx // 512, idx % 128 // 32])


BF16 = ml_dtypes.bfloat16


def bf(x):
    return np.asarray(x, np.float32).astype(BF16)


def f64(x):
    return np.asarray(x).astype(np.float64)


E2M1 = np.array([0.0, 0.5, 1.0, 1.5, 2.0, 3.0, 4.0, 6.0, -0.0, -0.5, -1.0, -1.5, -2.0, -3.0, -4.0, -6.0])


def pack_weight(w, fmt):
    k, n = w.shape
    w = f64(bf(w)).reshape(k // 32, 32, n)
    amax = np.abs(w).max(1)
    if fmt == "e4m3":
        byte = np.frexp(amax)[1] - 1 + 127 - 7
    else:
        mant, ex = np.frexp(amax / 6.0)
        byte = np.where(mant > 0.5, ex, ex - 1) + 127
    byte = np.clip(np.where(amax > 0, byte, 1), 1, 254)
    scaled = (w * np.exp2(127.0 - byte)[:, None, :]).reshape(k, n).astype(np.float32)
    by_word = np.ascontiguousarray(scaled.reshape(k // 512, 128, 4, n).transpose(0, 1, 3, 2))
    if fmt == "e4m3":
        words = by_word.astype(ml_dtypes.float8_e4m3fn).view(np.uint8)
    else:
        c = by_word.astype(ml_dtypes.float4_e2m1fn).view(np.uint8) & 0xF
        words = c[..., 0::2] | (c[..., 1::2] << 4)
    return np.ascontiguousarray(words), np.ascontiguousarray(byte.astype(np.uint8).reshape(k // 512, 16, n))


def unpack_weight(words, scales, fmt):
    g, p, n, _ = words.shape
    if fmt == "e4m3":
        vals = np.ascontiguousarray(words).view(ml_dtypes.float8_e4m3fn).astype(np.float64)
    else:
        nib = np.empty((g, p, n, 4), np.uint8)
        nib[..., 0::2] = words & 0xF
        nib[..., 1::2] = words >> 4
        vals = E2M1[nib]
    vals = vals * np.repeat(np.exp2(scales.astype(np.float64) - 127.0), 8, axis=1)[..., None]
    return vals.transpose(0, 1, 3, 2).reshape(g * 512, n)


N, K, H, A = 2048, 2, 256, 10
D = K * H
T = A * H
FMT = "e4m3"


def sigmoid(v):
    return 1.0 / (1.0 + np.exp(-v))


def setup_inputs():
    s = mx_kscale(D)
    h_mail = np.random.standard_normal((N, K, H)) * s.reshape(K, H)
    c_mail = np.random.standard_normal((N, K, H))
    U_f_w = np.random.standard_normal((T, T)) / np.sqrt(D)
    U_f_w[:D] = U_f_w[:D] / s[:, None]
    U_f_b = np.random.standard_normal(T) * 0.5
    U_iou_w = np.random.standard_normal((3 * H, T)) / np.sqrt(D)
    U_iou_w[:, :D] = U_iou_w[:, :D] / s
    b_iou = np.random.standard_normal((1, 3 * H)) * 0.3
    U_f_w_words, U_f_w_scales = pack_weight(U_f_w, FMT)
    U_iou_w_words, U_iou_w_scales = pack_weight(np.ascontiguousarray(U_iou_w.T), FMT)
    return {"h_mail": bf(h_mail), "c_mail": bf(c_mail), "U_f_w_words": U_f_w_words, "U_f_w_scales": U_f_w_scales, "U_f_b": bf(U_f_b), "U_iou_w_words": U_iou_w_words, "U_iou_w_scales": U_iou_w_scales, "b_iou": bf(b_iou)}


def reference(h_mail, c_mail, U_f_w_words, U_f_w_scales, U_f_b, U_iou_w_words, U_iou_w_scales, b_iou):
    n, k, h = h_mail.shape
    d = k * h
    hq = mxq(f64(h_mail).reshape(n, d), 1, "e4m3")
    f = sigmoid((hq @ unpack_weight(U_f_w_words, U_f_w_scales, FMT)[:d, :d]) + f64(U_f_b)[:d])
    c_red = np.sum(f.reshape(n, k, h) * f64(c_mail), axis=1)
    iou = (hq @ unpack_weight(U_iou_w_words, U_iou_w_scales, FMT)[:d, :]) + f64(b_iou)
    i, o, u = np.split(iou, 3, axis=1)
    c = sigmoid(i) * np.tanh(u) + c_red
    h_out = sigmoid(o) * np.tanh(c)
    return h_out, c

@@ -1,0 +1,207 @@
+from contextlib import ExitStack
+
+import concourse.mybir as mybir
+from concourse.masks import make_identity
+
+F32 = mybir.dt.float32
+BF16 = mybir.dt.bfloat16
+I32 = mybir.dt.int32
+U32 = mybir.dt.uint32
+U8 = mybir.dt.uint8
+FP8X4 = mybir.dt.float8_e4m3fn_x4
+ACT = mybir.ActivationFunctionType
+ALU = mybir.AluOpType
+
+P = 128
+PACK = 4
+NODES = 2048
+CHILDREN = 2
+H = 256
+D = CHILDREN * H
+W_COLS = D + 3 * H
+FEATURE_TILES = W_COLS // P
+HALVES = H // P
+
+NODE_TILES = NODES // P
+CHUNK = 512
+CHUNK_TILES = CHUNK // P
+N_CHUNKS = NODES // CHUNK
+PAIRS = CHUNK_TILES // 2
+
+F_TILE = 0
+I_TILE = D // P
+O_TILE = I_TILE + HALVES
+U_TILE = O_TILE + HALVES
+
+FLOPS = 2 * NODES * D * W_COLS
+BYTES = (
+    2 * NODES * D * 2
+    + D * W_COLS + (D // 32) * W_COLS + 2 * W_COLS
+    + 2 * NODES * H * 4
+)
+
+
+def tile_treelstmcell_kernel(
+    tc, h_mail, c_mail, U_f_w_words, U_f_w_scales, U_f_b, U_iou_w_words, U_iou_w_scales, b_iou, out_0, out_1
+):
+    nc = tc.nc
+    h_view = h_mail.rearrange("(p t) k j -> p t (k j)", t=NODE_TILES)
+    cm_view = c_mail.rearrange("(p t) k j -> p t k j", t=NODE_TILES)
+    h_out_view = out_0.rearrange("(p t) j -> p t j", t=NODE_TILES)
+    c_out_view = out_1.rearrange("(p t) j -> p t j", t=NODE_TILES)
+
+    with ExitStack() as ctx:
+        const = ctx.enter_context(tc.tile_pool(name="const", bufs=1))
+        loads = ctx.enter_context(tc.tile_pool(name="loads", bufs=N_CHUNKS))
+        quant = ctx.enter_context(tc.tile_pool(name="quant", bufs=2))
+        gates = ctx.enter_context(tc.tile_pool(name="gates", bufs=2))
+        rows = ctx.enter_context(tc.tile_pool(name="rows", bufs=3))
+        mx_psum = ctx.enter_context(tc.psum_pool(name="mx_psum", bufs=4))
+        tp_psum = ctx.enter_context(tc.psum_pool(name="tp_psum", bufs=4))
+
+        ident = const.tile([P, P], F32, name="ident")
+        make_identity(nc, ident[:])
+
+        bias_rows = const.tile([P, P], BF16, name="bias_rows")
+        nc.vector.memset(bias_rows[:], 0.0)
+        w_scales = const.tile([P, W_COLS], U8, name="w_scales", align_bytes=64)
+        nc.vector.memset(w_scales[:].bitcast(I32), 0)
+        w_codes = const.tile([P, W_COLS], U32, name="w_codes", align_bytes=64)
+
+        h_sb = []
+        cm_sb = []
+        for c in range(N_CHUNKS):
+            h_sb.append(loads.tile([P, CHUNK_TILES, D], BF16, name="h_sb", tag="h"))
+            cm_sb.append(loads.tile([P, CHUNK_TILES, CHILDREN, H], BF16, name="cm_sb", tag="cm"))
+
+        def load_h(c):
+            nc.sync.dma_start(out=h_sb[c][:], in_=h_view[:, c * CHUNK_TILES : (c + 1) * CHUNK_TILES, :])
+
+        def load_cm(c):
+            nc.sync.dma_start(out=cm_sb[c][:], in_=cm_view[:, c * CHUNK_TILES : (c + 1) * CHUNK_TILES, :, :])
+
+        def load_scales(dram, first_col, cols):
+            for quad in range(4):
+                nc.sync.dma_start(
+                    out=w_scales[32 * quad : 32 * quad + 4, first_col : first_col + cols].bitcast(I32),
+                    in_=dram[0, 4 * quad : 4 * quad + 4, 0:cols].bitcast(I32),
+                )
+
+        def load_codes(dram, first_col, cols):
+            nc.sync.dma_start(
+                out=w_codes[:, first_col : first_col + cols].bitcast(I32),
+                in_=dram[0].rearrange("p n t -> p (n t)")[:, 0 : cols * PACK].bitcast(I32),
+            )
+
+        load_h(0)
+        nc.sync.dma_start(out=bias_rows[0:I_TILE, :], in_=U_f_b[0:D].rearrange("(m p) -> m p", p=P))
+        nc.sync.dma_start(out=bias_rows[I_TILE:FEATURE_TILES, :], in_=b_iou.rearrange("o (m p) -> (o m) p", p=P))
+        load_scales(U_iou_w_scales, D, 3 * H)
+        load_codes(U_iou_w_words, D, 3 * H)
+        load_scales(U_f_w_scales, 0, D)
+        load_codes(U_f_w_words, 0, D)
+        load_h(1)
+        load_cm(0)
+        load_h(2)
+        load_cm(1)
+        load_h(3)
+        load_cm(2)
+        load_cm(3)
+
+        bias_rows_f32 = const.tile([P, P], F32, name="bias_rows_f32")
+        nc.vector.tensor_copy(out=bias_rows_f32[:], in_=bias_rows[:])
+        bias_bank = tp_psum.tile([P, 2, H], F32, name="bias_bank", tag="tp")
+        nc.tensor.transpose(out=bias_bank[:, 0, 0:P], in_=bias_rows_f32[:], identity=ident[:])
+        bias_sb = const.tile([P, FEATURE_TILES], F32, name="bias_sb")
+        nc.vector.tensor_copy(out=bias_sb[:], in_=bias_bank[:, 0, 0:FEATURE_TILES])
+
+        def quantise_chunk(c):
+            grouped = quant.tile([P, CHUNK * PACK], BF16, name="grouped", align_bytes=64)
+            grouped_words = grouped[:].bitcast(F32).rearrange("p (n u) -> p n u", u=2)
+            for pair in range(PAIRS):
+                h_bank = tp_psum.tile([P, 2, 2 * P], F32, name="h_bank", tag="tp")
+                for tl in range(2):
+                    words = h_sb[c][:, 2 * pair + tl, :].bitcast(F32)
+                    for u in range(2):
+                        nc.tensor.transpose(
+                            out=h_bank[:, u, tl * P : (tl + 1) * P], in_=words[:, u : D // 2 : 2], identity=ident[:]
+                        )
+                nc.vector.tensor_copy(
+                    out=grouped_words[:, pair * 2 * P : (pair + 1) * 2 * P, :],
+                    in_=h_bank[:].rearrange("p u n -> p n u"),
+                )
+            h_codes = quant.tile([P, CHUNK], U32, name="h_codes", align_bytes=64)
+            h_scales = quant.tile([P, CHUNK], U8, name="h_scales", align_bytes=64)
+            nc.vector.quantize_mx(out=h_codes[:].bitcast(FP8X4), scales=h_scales[:], in_=grouped[:])
+            return h_codes, h_scales
+
+        def gate_pass(h_q, m, func, dest):
+            h_codes, h_scales = h_q
+            bank = mx_psum.tile([P, CHUNK], F32, name="bank", tag="mx")
+            nc.tensor.matmul_mx(
+                out=bank[:],
+                lhsT=w_codes[:, m * P : (m + 1) * P].bitcast(FP8X4),
+                lhsT_scale=w_scales[:, m * P : (m + 1) * P],
+                rhs=h_codes[:].bitcast(FP8X4),
+                rhs_scale=h_scales[:],
+                start=True,
+                stop=True,
+            )
+            nc.scalar.activation(out=dest, in_=bank[:], func=func, bias=bias_sb[:, m : m + 1], scale=1.0)
+
+        def to_node_rows(src, pair):
+            t_bank = tp_psum.tile([P, 2, H], F32, name="t_bank", tag="tp")
+            for tl in range(2):
+                t = 2 * pair + tl
+                for half in range(HALVES):
+                    nc.tensor.transpose(
+                        out=t_bank[:, tl, half * P : (half + 1) * P],
+                        in_=src[:, half, t * P : (t + 1) * P],
+                        identity=ident[:],
+                    )
+            return t_bank
+
+        h_q = {0: quantise_chunk(0)}
+        for c in range(N_CHUNKS):
+            i_act = gates.tile([P, HALVES, CHUNK], F32, name="i_act")
+            u_act = gates.tile([P, HALVES, CHUNK], F32, name="u_act")
+            iu_act = gates.tile([P, HALVES, CHUNK], F32, name="iu_act")
+            for half in range(HALVES):
+                gate_pass(h_q[c], I_TILE + half, ACT.Sigmoid, i_act[:, half, :])
+                gate_pass(h_q[c], U_TILE + half, ACT.Tanh, u_act[:, half, :])
+                nc.gpsimd.tensor_tensor(
+                    out=iu_act[:, half, :], in0=i_act[:, half, :], in1=u_act[:, half, :], op=ALU.mult
+                )
+            if c + 1 < N_CHUNKS:
+                h_q[c + 1] = quantise_chunk(c + 1)
+            f_act = []
+            for child in range(CHILDREN):
+                f_child = gates.tile([P, HALVES, CHUNK], F32, name="f_child", tag="f%d" % child)
+                for half in range(HALVES):
+                    gate_pass(h_q[c], F_TILE + child * HALVES + half, ACT.Sigmoid, f_child[:, half, :])
+                f_act.append(f_child)
+            o_act = gates.tile([P, HALVES, CHUNK], F32, name="o_act")
+            for half in range(HALVES):
+                gate_pass(h_q[c], O_TILE + half, ACT.Sigmoid, o_act[:, half, :])
+
+            c_rows = rows.tile([P, CHUNK_TILES, H], F32, name="c_rows")
+            h_rows = rows.tile([P, CHUNK_TILES, H], F32, name="h_rows")
+            for pair in range(PAIRS):
+                ts = slice(2 * pair, 2 * pair + 2)
+                f0_bank = to_node_rows(f_act[0], pair)
+                kept0 = rows.tile([P, 2, H], F32, name="kept0")
+                nc.vector.tensor_tensor(out=kept0[:], in0=f0_bank[:], in1=cm_sb[c][:, ts, 0, :], op=ALU.mult)
+                iu_bank = to_node_rows(iu_act, pair)
+                partial = rows.tile([P, 2, H], F32, name="partial")
+                nc.vector.tensor_tensor(out=partial[:], in0=iu_bank[:], in1=kept0[:], op=ALU.add)
+                f1_bank = to_node_rows(f_act[1], pair)
+                kept1 = rows.tile([P, 2, H], F32, name="kept1")
+                nc.vector.tensor_tensor(out=kept1[:], in0=f1_bank[:], in1=cm_sb[c][:, ts, 1, :], op=ALU.mult)
+                nc.gpsimd.tensor_tensor(out=c_rows[:, ts, :], in0=partial[:], in1=kept1[:], op=ALU.add)
+                tanh_c = rows.tile([P, 2, H], F32, name="tanh_c")
+                nc.scalar.activation(out=tanh_c[:], in_=c_rows[:, ts, :], func=ACT.Tanh)
+                o_bank = to_node_rows(o_act, pair)
+                nc.vector.tensor_tensor(out=h_rows[:, ts, :], in0=o_bank[:], in1=tanh_c[:], op=ALU.mult)
+            chunk_tiles = slice(c * CHUNK_TILES, (c + 1) * CHUNK_TILES)
+            nc.sync.dma_start(out=c_out_view[:, chunk_tiles, :], in_=c_rows[:])
+            nc.sync.dma_start(out=h_out_view[:, chunk_tiles, :], in_=h_rows[:])

@@ -58,6 +58,7 @@ def tile_treelstmcell_kernel(
         rows = ctx.enter_context(tc.tile_pool(name="rows", bufs=3))
         mx_psum = ctx.enter_context(tc.psum_pool(name="mx_psum", bufs=4))
         tp_psum = ctx.enter_context(tc.psum_pool(name="tp_psum", bufs=4))
+        ctx.enter_context(tc.manual_schedule())
 
         ident = const.tile([P, P], F32, name="ident")
         make_identity(nc, ident[:])
@@ -135,20 +136,6 @@ def tile_treelstmcell_kernel(
             nc.vector.quantize_mx(out=h_codes[:].bitcast(FP8X4), scales=h_scales[:], in_=grouped[:])
             return h_codes, h_scales
 
-        def gate_pass(h_q, m, func, dest):
-            h_codes, h_scales = h_q
-            bank = mx_psum.tile([P, CHUNK], F32, name="bank", tag="mx")
-            nc.tensor.matmul_mx(
-                out=bank[:],
-                lhsT=w_codes[:, m * P : (m + 1) * P].bitcast(FP8X4),
-                lhsT_scale=w_scales[:, m * P : (m + 1) * P],
-                rhs=h_codes[:].bitcast(FP8X4),
-                rhs_scale=h_scales[:],
-                start=True,
-                stop=True,
-            )
-            nc.scalar.activation(out=dest, in_=bank[:], func=func, bias=bias_sb[:, m : m + 1], scale=1.0)
-
         def to_node_rows(src, pair):
             t_bank = tp_psum.tile([P, 2, H], F32, name="t_bank", tag="tp")
             for tl in range(2):
@@ -161,47 +148,123 @@ def tile_treelstmcell_kernel(
                     )
             return t_bank
 
-        h_q = {0: quantise_chunk(0)}
-        for c in range(N_CHUNKS):
-            i_act = gates.tile([P, HALVES, CHUNK], F32, name="i_act")
-            u_act = gates.tile([P, HALVES, CHUNK], F32, name="u_act")
-            iu_act = gates.tile([P, HALVES, CHUNK], F32, name="iu_act")
-            for half in range(HALVES):
-                gate_pass(h_q[c], I_TILE + half, ACT.Sigmoid, i_act[:, half, :])
-                gate_pass(h_q[c], U_TILE + half, ACT.Tanh, u_act[:, half, :])
-                nc.gpsimd.tensor_tensor(
-                    out=iu_act[:, half, :], in0=i_act[:, half, :], in1=u_act[:, half, :], op=ALU.mult
-                )
-            if c + 1 < N_CHUNKS:
-                h_q[c + 1] = quantise_chunk(c + 1)
-            f_act = []
-            for child in range(CHILDREN):
-                f_child = gates.tile([P, HALVES, CHUNK], F32, name="f_child", tag="f%d" % child)
-                for half in range(HALVES):
-                    gate_pass(h_q[c], F_TILE + child * HALVES + half, ACT.Sigmoid, f_child[:, half, :])
-                f_act.append(f_child)
-            o_act = gates.tile([P, HALVES, CHUNK], F32, name="o_act")
-            for half in range(HALVES):
-                gate_pass(h_q[c], O_TILE + half, ACT.Sigmoid, o_act[:, half, :])
+        ROUNDS = 5
+        IU_ROUNDS = (2, 3)
+        SIGMOID_ROUNDS = {0: ("f0", F_TILE), 1: ("f1", F_TILE + HALVES), 4: ("o", O_TILE)}
+        h_q = {}
+        banks = {}
+        gate = {}
+        node = {}
 
-            c_rows = rows.tile([P, CHUNK_TILES, H], F32, name="c_rows")
-            h_rows = rows.tile([P, CHUNK_TILES, H], F32, name="h_rows")
+        def feature_tiles(r):
+            if r in IU_ROUNDS:
+                return (I_TILE + r - IU_ROUNDS[0], U_TILE + r - IU_ROUNDS[0])
+            return (SIGMOID_ROUNDS[r][1], SIGMOID_ROUNDS[r][1] + 1)
+
+        def multiply(c, r):
+            h_codes, h_scales = h_q[c]
+            banks[(c, r)] = []
+            for m in feature_tiles(r):
+                bank = mx_psum.tile([P, CHUNK], F32, name="bank", tag="mx")
+                nc.tensor.matmul_mx(
+                    out=bank[:],
+                    lhsT=w_codes[:, m * P : (m + 1) * P].bitcast(FP8X4),
+                    lhsT_scale=w_scales[:, m * P : (m + 1) * P],
+                    rhs=h_codes[:].bitcast(FP8X4),
+                    rhs_scale=h_scales[:],
+                    start=True,
+                    stop=True,
+                )
+                banks[(c, r)].append(bank)
+
+        def new_gate(c, name):
+            gate[(c, name)] = gates.tile([P, HALVES, CHUNK], F32, name="gate_" + name)
+
+        def activate(c, r):
+            first, second = feature_tiles(r)
+            if r in IU_ROUNDS:
+                half = r - IU_ROUNDS[0]
+                if half == 0:
+                    for name in ("i", "u", "iu"):
+                        new_gate(c, name)
+                dests = (gate[(c, "i")][:, half, :], gate[(c, "u")][:, half, :])
+                funcs = (ACT.Sigmoid, ACT.Tanh)
+            else:
+                name = SIGMOID_ROUNDS[r][0]
+                new_gate(c, name)
+                dests = (gate[(c, name)][:, 0, :], gate[(c, name)][:, 1, :])
+                funcs = (ACT.Sigmoid, ACT.Sigmoid)
+            for bank, m, func, dest in zip(banks[(c, r)], (first, second), funcs, dests):
+                nc.scalar.activation(out=dest, in_=bank[:], func=func, bias=bias_sb[:, m : m + 1], scale=1.0)
+            if r in IU_ROUNDS:
+                nc.gpsimd.tensor_tensor(out=gate[(c, "iu")][:, half, :], in0=dests[0], in1=dests[1], op=ALU.mult)
+
+        def new_node(c, name):
+            node[(c, name)] = rows.tile([P, CHUNK_TILES, H], F32, name="node_" + name)
+
+        def node_banks(c, name):
+            return [(slice(2 * pair, 2 * pair + 2), to_node_rows(gate[(c, name)], pair)) for pair in range(PAIRS)]
+
+        def keep_child(c, child):
+            kept = "kept%d" % child
+            new_node(c, kept)
+            if child == 1:
+                new_node(c, "c_red")
+            for ts, t_bank in node_banks(c, "f%d" % child):
+                nc.vector.tensor_tensor(
+                    out=node[(c, kept)][:, ts, :], in0=t_bank[:], in1=cm_sb[c][:, ts, child, :], op=ALU.mult
+                )
+                if child == 1:
+                    nc.gpsimd.tensor_tensor(
+                        out=node[(c, "c_red")][:, ts, :],
+                        in0=node[(c, "kept0")][:, ts, :],
+                        in1=node[(c, "kept1")][:, ts, :],
+                        op=ALU.add,
+                    )
+
+        def new_cell(c):
+            new_node(c, "c")
+            for ts, t_bank in node_banks(c, "iu"):
+                nc.vector.tensor_tensor(
+                    out=node[(c, "c")][:, ts, :], in0=t_bank[:], in1=node[(c, "c_red")][:, ts, :], op=ALU.add
+                )
+            nc.sync.dma_start(out=c_out_view[:, c * CHUNK_TILES : (c + 1) * CHUNK_TILES, :], in_=node[(c, "c")][:])
+
+        def squash_cell(c):
+            new_node(c, "tanh_c")
             for pair in range(PAIRS):
                 ts = slice(2 * pair, 2 * pair + 2)
-                f0_bank = to_node_rows(f_act[0], pair)
-                kept0 = rows.tile([P, 2, H], F32, name="kept0")
-                nc.vector.tensor_tensor(out=kept0[:], in0=f0_bank[:], in1=cm_sb[c][:, ts, 0, :], op=ALU.mult)
-                iu_bank = to_node_rows(iu_act, pair)
-                partial = rows.tile([P, 2, H], F32, name="partial")
-                nc.vector.tensor_tensor(out=partial[:], in0=iu_bank[:], in1=kept0[:], op=ALU.add)
-                f1_bank = to_node_rows(f_act[1], pair)
-                kept1 = rows.tile([P, 2, H], F32, name="kept1")
-                nc.vector.tensor_tensor(out=kept1[:], in0=f1_bank[:], in1=cm_sb[c][:, ts, 1, :], op=ALU.mult)
-                nc.gpsimd.tensor_tensor(out=c_rows[:, ts, :], in0=partial[:], in1=kept1[:], op=ALU.add)
-                tanh_c = rows.tile([P, 2, H], F32, name="tanh_c")
-                nc.scalar.activation(out=tanh_c[:], in_=c_rows[:, ts, :], func=ACT.Tanh)
-                o_bank = to_node_rows(o_act, pair)
-                nc.vector.tensor_tensor(out=h_rows[:, ts, :], in0=o_bank[:], in1=tanh_c[:], op=ALU.mult)
-            chunk_tiles = slice(c * CHUNK_TILES, (c + 1) * CHUNK_TILES)
-            nc.sync.dma_start(out=c_out_view[:, chunk_tiles, :], in_=c_rows[:])
-            nc.sync.dma_start(out=h_out_view[:, chunk_tiles, :], in_=h_rows[:])
+                nc.scalar.activation(out=node[(c, "tanh_c")][:, ts, :], in_=node[(c, "c")][:, ts, :], func=ACT.Tanh)
+
+        def new_hidden(c):
+            new_node(c, "h")
+            for ts, t_bank in node_banks(c, "o"):
+                nc.vector.tensor_tensor(
+                    out=node[(c, "h")][:, ts, :], in0=t_bank[:], in1=node[(c, "tanh_c")][:, ts, :], op=ALU.mult
+                )
+            nc.sync.dma_start(out=h_out_view[:, c * CHUNK_TILES : (c + 1) * CHUNK_TILES, :], in_=node[(c, "h")][:])
+
+        h_q[0] = quantise_chunk(0)
+        multiply(0, 0)
+        for c in range(N_CHUNKS):
+            for r in range(ROUNDS):
+                if r + 1 < ROUNDS:
+                    multiply(c, r + 1)
+                elif c + 1 < N_CHUNKS:
+                    multiply(c + 1, 0)
+                activate(c, r)
+                if r == 0 and c + 1 < N_CHUNKS:
+                    h_q[c + 1] = quantise_chunk(c + 1)
+                if r == 1 and c > 0:
+                    new_cell(c - 1)
+                if r == 2:
+                    keep_child(c, 0)
+                if r == 3:
+                    keep_child(c, 1)
+                    if c > 0:
+                        squash_cell(c - 1)
+                if r == 4 and c > 0:
+                    new_hidden(c - 1)
+        new_cell(N_CHUNKS - 1)
+        squash_cell(N_CHUNKS - 1)
+        new_hidden(N_CHUNKS - 1)

@@ -53,7 +53,7 @@ def tile_treelstmcell_kernel(
     with ExitStack() as ctx:
         const = ctx.enter_context(tc.tile_pool(name="const", bufs=1))
         loads = ctx.enter_context(tc.tile_pool(name="loads", bufs=N_CHUNKS))
-        quant = ctx.enter_context(tc.tile_pool(name="quant", bufs=2))
+        quant = ctx.enter_context(tc.tile_pool(name="quant", bufs=3))
         gates = ctx.enter_context(tc.tile_pool(name="gates", bufs=2))
         rows = ctx.enter_context(tc.tile_pool(name="rows", bufs=3))
         mx_psum = ctx.enter_context(tc.psum_pool(name="mx_psum", bufs=4))
@@ -95,17 +95,17 @@ def tile_treelstmcell_kernel(
             )
 
         load_h(0)
+        load_h(1)
         nc.sync.dma_start(out=bias_rows[0:I_TILE, :], in_=U_f_b[0:D].rearrange("(m p) -> m p", p=P))
         nc.sync.dma_start(out=bias_rows[I_TILE:FEATURE_TILES, :], in_=b_iou.rearrange("o (m p) -> (o m) p", p=P))
-        load_scales(U_iou_w_scales, D, 3 * H)
-        load_codes(U_iou_w_words, D, 3 * H)
         load_scales(U_f_w_scales, 0, D)
         load_codes(U_f_w_words, 0, D)
-        load_h(1)
-        load_cm(0)
+        load_scales(U_iou_w_scales, D, 3 * H)
+        load_codes(U_iou_w_words, D, 3 * H)
         load_h(2)
-        load_cm(1)
+        load_cm(0)
         load_h(3)
+        load_cm(1)
         load_cm(2)
         load_cm(3)
 
@@ -127,10 +127,8 @@ def tile_treelstmcell_kernel(
                         nc.tensor.transpose(
                             out=h_bank[:, u, tl * P : (tl + 1) * P], in_=words[:, u : D // 2 : 2], identity=ident[:]
                         )
-                nc.vector.tensor_copy(
-                    out=grouped_words[:, pair * 2 * P : (pair + 1) * 2 * P, :],
-                    in_=h_bank[:].rearrange("p u n -> p n u"),
-                )
+                nodes = slice(pair * 2 * P, (pair + 1) * 2 * P)
+                nc.vector.tensor_copy(out=grouped_words[:, nodes, :], in_=h_bank[:].rearrange("p u n -> p n u"))
             h_codes = quant.tile([P, CHUNK], U32, name="h_codes", align_bytes=64)
             h_scales = quant.tile([P, CHUNK], U8, name="h_scales", align_bytes=64)
             nc.vector.quantize_mx(out=h_codes[:].bitcast(FP8X4), scales=h_scales[:], in_=grouped[:])
@@ -203,14 +201,17 @@ def tile_treelstmcell_kernel(
             node[(c, name)] = rows.tile([P, CHUNK_TILES, H], F32, name="node_" + name)
 
         def node_banks(c, name):
-            return [(slice(2 * pair, 2 * pair + 2), to_node_rows(gate[(c, name)], pair)) for pair in range(PAIRS)]
+            return [(pair, slice(2 * pair, 2 * pair + 2), to_node_rows(gate[(c, name)], pair)) for pair in range(PAIRS)]
+
+        def dram_tiles(c, pair):
+            return slice(c * CHUNK_TILES + 2 * pair, c * CHUNK_TILES + 2 * pair + 2)
 
         def keep_child(c, child):
             kept = "kept%d" % child
             new_node(c, kept)
             if child == 1:
                 new_node(c, "c_red")
-            for ts, t_bank in node_banks(c, "f%d" % child):
+            for pair, ts, t_bank in node_banks(c, "f%d" % child):
                 nc.vector.tensor_tensor(
                     out=node[(c, kept)][:, ts, :], in0=t_bank[:], in1=cm_sb[c][:, ts, child, :], op=ALU.mult
                 )
@@ -224,11 +225,11 @@ def tile_treelstmcell_kernel(
 
         def new_cell(c):
             new_node(c, "c")
-            for ts, t_bank in node_banks(c, "iu"):
+            for pair, ts, t_bank in node_banks(c, "iu"):
                 nc.vector.tensor_tensor(
                     out=node[(c, "c")][:, ts, :], in0=t_bank[:], in1=node[(c, "c_red")][:, ts, :], op=ALU.add
                 )
-            nc.sync.dma_start(out=c_out_view[:, c * CHUNK_TILES : (c + 1) * CHUNK_TILES, :], in_=node[(c, "c")][:])
+                nc.sync.dma_start(out=c_out_view[:, dram_tiles(c, pair), :], in_=node[(c, "c")][:, ts, :])
 
         def squash_cell(c):
             new_node(c, "tanh_c")
@@ -238,13 +239,14 @@ def tile_treelstmcell_kernel(
 
         def new_hidden(c):
             new_node(c, "h")
-            for ts, t_bank in node_banks(c, "o"):
+            for pair, ts, t_bank in node_banks(c, "o"):
                 nc.vector.tensor_tensor(
                     out=node[(c, "h")][:, ts, :], in0=t_bank[:], in1=node[(c, "tanh_c")][:, ts, :], op=ALU.mult
                 )
-            nc.sync.dma_start(out=h_out_view[:, c * CHUNK_TILES : (c + 1) * CHUNK_TILES, :], in_=node[(c, "h")][:])
+                nc.sync.dma_start(out=h_out_view[:, dram_tiles(c, pair), :], in_=node[(c, "h")][:, ts, :])
 
         h_q[0] = quantise_chunk(0)
+        h_q[1] = quantise_chunk(1)
         multiply(0, 0)
         for c in range(N_CHUNKS):
             for r in range(ROUNDS):
@@ -253,8 +255,8 @@ def tile_treelstmcell_kernel(
                 elif c + 1 < N_CHUNKS:
                     multiply(c + 1, 0)
                 activate(c, r)
-                if r == 0 and c + 1 < N_CHUNKS:
-                    h_q[c + 1] = quantise_chunk(c + 1)
+                if r == 0 and c + 2 < N_CHUNKS:
+                    h_q[c + 2] = quantise_chunk(c + 2)
                 if r == 1 and c > 0:
                     new_cell(c - 1)
                 if r == 2:

@@ -53,7 +53,7 @@ def tile_treelstmcell_kernel(
     with ExitStack() as ctx:
         const = ctx.enter_context(tc.tile_pool(name="const", bufs=1))
         loads = ctx.enter_context(tc.tile_pool(name="loads", bufs=N_CHUNKS))
-        quant = ctx.enter_context(tc.tile_pool(name="quant", bufs=3))
+        quant = ctx.enter_context(tc.tile_pool(name="quant", bufs=2))
         gates = ctx.enter_context(tc.tile_pool(name="gates", bufs=2))
         rows = ctx.enter_context(tc.tile_pool(name="rows", bufs=3))
         mx_psum = ctx.enter_context(tc.psum_pool(name="mx_psum", bufs=4))
@@ -63,10 +63,10 @@ def tile_treelstmcell_kernel(
         ident = const.tile([P, P], F32, name="ident")
         make_identity(nc, ident[:])
 
-        bias_rows = const.tile([P, P], BF16, name="bias_rows")
-        nc.vector.memset(bias_rows[:], 0.0)
         w_scales = const.tile([P, W_COLS], U8, name="w_scales", align_bytes=64)
         nc.vector.memset(w_scales[:].bitcast(I32), 0)
+        bias_rows = const.tile([P, P], BF16, name="bias_rows")
+        nc.vector.memset(bias_rows[:], 0.0)
         w_codes = const.tile([P, W_COLS], U32, name="w_codes", align_bytes=64)
 
         h_sb = []
@@ -95,26 +95,19 @@ def tile_treelstmcell_kernel(
             )
 
         load_h(0)
-        load_h(1)
-        nc.sync.dma_start(out=bias_rows[0:I_TILE, :], in_=U_f_b[0:D].rearrange("(m p) -> m p", p=P))
-        nc.sync.dma_start(out=bias_rows[I_TILE:FEATURE_TILES, :], in_=b_iou.rearrange("o (m p) -> (o m) p", p=P))
-        load_scales(U_f_w_scales, 0, D)
         load_codes(U_f_w_words, 0, D)
-        load_scales(U_iou_w_scales, D, 3 * H)
+        load_scales(U_f_w_scales, 0, D)
+        nc.scalar.dma_start(out=bias_rows[0:I_TILE, :], in_=U_f_b[0:D].rearrange("(m p) -> m p", p=P))
+        nc.scalar.dma_start(out=bias_rows[I_TILE:FEATURE_TILES, :], in_=b_iou.rearrange("o (m p) -> (o m) p", p=P))
         load_codes(U_iou_w_words, D, 3 * H)
-        load_h(2)
+        load_h(1)
+        load_scales(U_iou_w_scales, D, 3 * H)
         load_cm(0)
-        load_h(3)
+        load_h(2)
         load_cm(1)
+        load_h(3)
         load_cm(2)
         load_cm(3)
-
-        bias_rows_f32 = const.tile([P, P], F32, name="bias_rows_f32")
-        nc.vector.tensor_copy(out=bias_rows_f32[:], in_=bias_rows[:])
-        bias_bank = tp_psum.tile([P, 2, H], F32, name="bias_bank", tag="tp")
-        nc.tensor.transpose(out=bias_bank[:, 0, 0:P], in_=bias_rows_f32[:], identity=ident[:])
-        bias_sb = const.tile([P, FEATURE_TILES], F32, name="bias_sb")
-        nc.vector.tensor_copy(out=bias_sb[:], in_=bias_bank[:, 0, 0:FEATURE_TILES])
 
         def quantise_chunk(c):
             grouped = quant.tile([P, CHUNK * PACK], BF16, name="grouped", align_bytes=64)
@@ -127,8 +120,10 @@ def tile_treelstmcell_kernel(
                         nc.tensor.transpose(
                             out=h_bank[:, u, tl * P : (tl + 1) * P], in_=words[:, u : D // 2 : 2], identity=ident[:]
                         )
-                nodes = slice(pair * 2 * P, (pair + 1) * 2 * P)
-                nc.vector.tensor_copy(out=grouped_words[:, nodes, :], in_=h_bank[:].rearrange("p u n -> p n u"))
+                nc.vector.tensor_copy(
+                    out=grouped_words[:, pair * 2 * P : (pair + 1) * 2 * P, :],
+                    in_=h_bank[:].rearrange("p u n -> p n u"),
+                )
             h_codes = quant.tile([P, CHUNK], U32, name="h_codes", align_bytes=64)
             h_scales = quant.tile([P, CHUNK], U8, name="h_scales", align_bytes=64)
             nc.vector.quantize_mx(out=h_codes[:].bitcast(FP8X4), scales=h_scales[:], in_=grouped[:])
@@ -245,8 +240,14 @@ def tile_treelstmcell_kernel(
                 )
                 nc.sync.dma_start(out=h_out_view[:, dram_tiles(c, pair), :], in_=node[(c, "h")][:, ts, :])
 
+        bias_rows_f32 = const.tile([P, P], F32, name="bias_rows_f32")
+        nc.vector.tensor_copy(out=bias_rows_f32[:], in_=bias_rows[:])
         h_q[0] = quantise_chunk(0)
-        h_q[1] = quantise_chunk(1)
+        bias_bank = tp_psum.tile([P, 2, H], F32, name="bias_bank", tag="tp")
+        nc.tensor.transpose(out=bias_bank[:, 0, 0:P], in_=bias_rows_f32[:], identity=ident[:])
+        bias_sb = const.tile([P, FEATURE_TILES], F32, name="bias_sb")
+        nc.vector.tensor_copy(out=bias_sb[:], in_=bias_bank[:, 0, 0:FEATURE_TILES])
+
         multiply(0, 0)
         for c in range(N_CHUNKS):
             for r in range(ROUNDS):
@@ -255,8 +256,8 @@ def tile_treelstmcell_kernel(
                 elif c + 1 < N_CHUNKS:
                     multiply(c + 1, 0)
                 activate(c, r)
-                if r == 0 and c + 2 < N_CHUNKS:
-                    h_q[c + 2] = quantise_chunk(c + 2)
+                if r == 0 and c + 1 < N_CHUNKS:
+                    h_q[c + 1] = quantise_chunk(c + 1)
                 if r == 1 and c > 0:
                     new_cell(c - 1)
                 if r == 2:

@@ -63,10 +63,10 @@ def tile_treelstmcell_kernel(
         ident = const.tile([P, P], F32, name="ident")
         make_identity(nc, ident[:])
 
-        w_scales = const.tile([P, W_COLS], U8, name="w_scales", align_bytes=64)
-        nc.vector.memset(w_scales[:].bitcast(I32), 0)
         bias_rows = const.tile([P, P], BF16, name="bias_rows")
         nc.vector.memset(bias_rows[:], 0.0)
+        w_scales = const.tile([P, W_COLS], U8, name="w_scales", align_bytes=64)
+        nc.vector.memset(w_scales[:].bitcast(I32), 0)
         w_codes = const.tile([P, W_COLS], U32, name="w_codes", align_bytes=64)
 
         h_sb = []
@@ -75,8 +75,10 @@ def tile_treelstmcell_kernel(
             h_sb.append(loads.tile([P, CHUNK_TILES, D], BF16, name="h_sb", tag="h"))
             cm_sb.append(loads.tile([P, CHUNK_TILES, CHILDREN, H], BF16, name="cm_sb", tag="cm"))
 
-        def load_h(c):
-            nc.sync.dma_start(out=h_sb[c][:], in_=h_view[:, c * CHUNK_TILES : (c + 1) * CHUNK_TILES, :])
+        def load_h(c, first=0, tiles=CHUNK_TILES):
+            nc.sync.dma_start(
+                out=h_sb[c][:, first : first + tiles, :], in_=h_view[:, c * CHUNK_TILES + first : c * CHUNK_TILES + first + tiles, :]
+            )
 
         def load_cm(c):
             nc.sync.dma_start(out=cm_sb[c][:], in_=cm_view[:, c * CHUNK_TILES : (c + 1) * CHUNK_TILES, :, :])
@@ -94,11 +96,12 @@ def tile_treelstmcell_kernel(
                 in_=dram[0].rearrange("p n t -> p (n t)")[:, 0 : cols * PACK].bitcast(I32),
             )
 
-        load_h(0)
-        load_codes(U_f_w_words, 0, D)
-        load_scales(U_f_w_scales, 0, D)
+        for pair in range(PAIRS):
+            load_h(0, 2 * pair, 2)
         nc.scalar.dma_start(out=bias_rows[0:I_TILE, :], in_=U_f_b[0:D].rearrange("(m p) -> m p", p=P))
         nc.scalar.dma_start(out=bias_rows[I_TILE:FEATURE_TILES, :], in_=b_iou.rearrange("o (m p) -> (o m) p", p=P))
+        load_codes(U_f_w_words, 0, D)
+        load_scales(U_f_w_scales, 0, D)
         load_codes(U_iou_w_words, D, 3 * H)
         load_h(1)
         load_scales(U_iou_w_scales, D, 3 * H)
@@ -109,25 +112,43 @@ def tile_treelstmcell_kernel(
         load_cm(2)
         load_cm(3)
 
-        def quantise_chunk(c):
-            grouped = quant.tile([P, CHUNK * PACK], BF16, name="grouped", align_bytes=64)
-            grouped_words = grouped[:].bitcast(F32).rearrange("p (n u) -> p n u", u=2)
-            for pair in range(PAIRS):
-                h_bank = tp_psum.tile([P, 2, 2 * P], F32, name="h_bank", tag="tp")
-                for tl in range(2):
-                    words = h_sb[c][:, 2 * pair + tl, :].bitcast(F32)
-                    for u in range(2):
-                        nc.tensor.transpose(
-                            out=h_bank[:, u, tl * P : (tl + 1) * P], in_=words[:, u : D // 2 : 2], identity=ident[:]
-                        )
-                nc.vector.tensor_copy(
-                    out=grouped_words[:, pair * 2 * P : (pair + 1) * 2 * P, :],
-                    in_=h_bank[:].rearrange("p u n -> p n u"),
-                )
+        grouped = {}
+        h_q = {}
+        PAIR_NODES = 2 * P
+
+        def new_h_tiles(c):
+            grouped[c] = quant.tile([P, CHUNK * PACK], BF16, name="grouped", align_bytes=64)
             h_codes = quant.tile([P, CHUNK], U32, name="h_codes", align_bytes=64)
             h_scales = quant.tile([P, CHUNK], U8, name="h_scales", align_bytes=64)
-            nc.vector.quantize_mx(out=h_codes[:].bitcast(FP8X4), scales=h_scales[:], in_=grouped[:])
-            return h_codes, h_scales
+            h_q[c] = (h_codes, h_scales)
+
+        def transpose_h(c, pair):
+            h_bank = tp_psum.tile([P, 2, 2 * P], F32, name="h_bank", tag="tp")
+            for tl in range(2):
+                words = h_sb[c][:, 2 * pair + tl, :].bitcast(F32)
+                for u in range(2):
+                    nc.tensor.transpose(out=h_bank[:, u, tl * P : (tl + 1) * P], in_=words[:, u : D // 2 : 2], identity=ident[:])
+            return h_bank
+
+        def group_h(c, pair, h_bank):
+            grouped_words = grouped[c][:].bitcast(F32).rearrange("p (n u) -> p n u", u=2)
+            nc.vector.tensor_copy(
+                out=grouped_words[:, pair * PAIR_NODES : (pair + 1) * PAIR_NODES, :], in_=h_bank[:].rearrange("p u n -> p n u")
+            )
+
+        def quantise(c, first_node, nodes):
+            h_codes, h_scales = h_q[c]
+            nc.vector.quantize_mx(
+                out=h_codes[:, first_node : first_node + nodes].bitcast(FP8X4),
+                scales=h_scales[:, first_node : first_node + nodes],
+                in_=grouped[c][:, first_node * PACK : (first_node + nodes) * PACK],
+            )
+
+        def quantise_chunk(c):
+            new_h_tiles(c)
+            for pair in range(PAIRS):
+                group_h(c, pair, transpose_h(c, pair))
+            quantise(c, 0, CHUNK)
 
         def to_node_rows(src, pair):
             t_bank = tp_psum.tile([P, 2, H], F32, name="t_bank", tag="tp")
@@ -144,7 +165,6 @@ def tile_treelstmcell_kernel(
         ROUNDS = 5
         IU_ROUNDS = (2, 3)
         SIGMOID_ROUNDS = {0: ("f0", F_TILE), 1: ("f1", F_TILE + HALVES), 4: ("o", O_TILE)}
-        h_q = {}
         banks = {}
         gate = {}
         node = {}
@@ -154,43 +174,55 @@ def tile_treelstmcell_kernel(
                 return (I_TILE + r - IU_ROUNDS[0], U_TILE + r - IU_ROUNDS[0])
             return (SIGMOID_ROUNDS[r][1], SIGMOID_ROUNDS[r][1] + 1)
 
+        def by_pairs(c, r):
+            return c == 0 and r < PAIRS
+
+        def passes(c, r):
+            if by_pairs(c, r):
+                return [(F_TILE + m, r * PAIR_NODES, PAIR_NODES, m // 2, (m % 2) * PAIR_NODES) for m in range(CHILDREN * HALVES)]
+            return [(m, 0, CHUNK, j, 0) for j, m in enumerate(feature_tiles(r))]
+
         def multiply(c, r):
             h_codes, h_scales = h_q[c]
-            banks[(c, r)] = []
-            for m in feature_tiles(r):
-                bank = mx_psum.tile([P, CHUNK], F32, name="bank", tag="mx")
+            banks[(c, r)] = [mx_psum.tile([P, CHUNK], F32, name="bank", tag="mx") for j in range(2)]
+            for m, first_node, nodes, j, first_col in passes(c, r):
                 nc.tensor.matmul_mx(
-                    out=bank[:],
+                    out=banks[(c, r)][j][:, first_col : first_col + nodes],
                     lhsT=w_codes[:, m * P : (m + 1) * P].bitcast(FP8X4),
                     lhsT_scale=w_scales[:, m * P : (m + 1) * P],
-                    rhs=h_codes[:].bitcast(FP8X4),
-                    rhs_scale=h_scales[:],
+                    rhs=h_codes[:, first_node : first_node + nodes].bitcast(FP8X4),
+                    rhs_scale=h_scales[:, first_node : first_node + nodes],
                     start=True,
                     stop=True,
                 )
-                banks[(c, r)].append(bank)
 
         def new_gate(c, name):
             gate[(c, name)] = gates.tile([P, HALVES, CHUNK], F32, name="gate_" + name)
 
+        GATE_OF_TILE = {}
+        for name, first in (("f0", F_TILE), ("f1", F_TILE + HALVES), ("i", I_TILE), ("o", O_TILE), ("u", U_TILE)):
+            for half in range(HALVES):
+                GATE_OF_TILE[first + half] = (name, half)
+
         def activate(c, r):
-            first, second = feature_tiles(r)
+            for m, first_node, nodes, j, first_col in passes(c, r):
+                name, half = GATE_OF_TILE[m]
+                if (c, name) not in gate:
+                    new_gate(c, name)
+                nc.scalar.activation(
+                    out=gate[(c, name)][:, half, first_node : first_node + nodes],
+                    in_=banks[(c, r)][j][:, first_col : first_col + nodes],
+                    func=ACT.Tanh if name == "u" else ACT.Sigmoid,
+                    bias=bias_sb[:, m : m + 1],
+                    scale=1.0,
+                )
             if r in IU_ROUNDS:
                 half = r - IU_ROUNDS[0]
                 if half == 0:
-                    for name in ("i", "u", "iu"):
-                        new_gate(c, name)
-                dests = (gate[(c, "i")][:, half, :], gate[(c, "u")][:, half, :])
-                funcs = (ACT.Sigmoid, ACT.Tanh)
-            else:
-                name = SIGMOID_ROUNDS[r][0]
-                new_gate(c, name)
-                dests = (gate[(c, name)][:, 0, :], gate[(c, name)][:, 1, :])
-                funcs = (ACT.Sigmoid, ACT.Sigmoid)
-            for bank, m, func, dest in zip(banks[(c, r)], (first, second), funcs, dests):
-                nc.scalar.activation(out=dest, in_=bank[:], func=func, bias=bias_sb[:, m : m + 1], scale=1.0)
-            if r in IU_ROUNDS:
-                nc.gpsimd.tensor_tensor(out=gate[(c, "iu")][:, half, :], in0=dests[0], in1=dests[1], op=ALU.mult)
+                    new_gate(c, "iu")
+                nc.gpsimd.tensor_tensor(
+                    out=gate[(c, "iu")][:, half, :], in0=gate[(c, "i")][:, half, :], in1=gate[(c, "u")][:, half, :], op=ALU.mult
+                )
 
         def new_node(c, name):
             node[(c, name)] = rows.tile([P, CHUNK_TILES, H], F32, name="node_" + name)
@@ -241,12 +273,17 @@ def tile_treelstmcell_kernel(
                 nc.sync.dma_start(out=h_out_view[:, dram_tiles(c, pair), :], in_=node[(c, "h")][:, ts, :])
 
         bias_rows_f32 = const.tile([P, P], F32, name="bias_rows_f32")
-        nc.vector.tensor_copy(out=bias_rows_f32[:], in_=bias_rows[:])
-        h_q[0] = quantise_chunk(0)
-        bias_bank = tp_psum.tile([P, 2, H], F32, name="bias_bank", tag="tp")
-        nc.tensor.transpose(out=bias_bank[:, 0, 0:P], in_=bias_rows_f32[:], identity=ident[:])
         bias_sb = const.tile([P, FEATURE_TILES], F32, name="bias_sb")
+        new_h_tiles(0)
+        h_banks = [transpose_h(0, pair) for pair in range(PAIRS)]
+        bias_bank = tp_psum.tile([P, 2, H], F32, name="bias_bank", tag="tp")
+        group_h(0, 0, h_banks[0])
+        nc.vector.tensor_copy(out=bias_rows_f32[:], in_=bias_rows[:])
+        nc.tensor.transpose(out=bias_bank[:, 0, 0:P], in_=bias_rows_f32[:], identity=ident[:])
+        quantise(0, 0, PAIR_NODES)
+        group_h(0, 1, h_banks[1])
         nc.vector.tensor_copy(out=bias_sb[:], in_=bias_bank[:, 0, 0:FEATURE_TILES])
+        quantise(0, PAIR_NODES, PAIR_NODES)
 
         multiply(0, 0)
         for c in range(N_CHUNKS):
@@ -257,7 +294,7 @@ def tile_treelstmcell_kernel(
                     multiply(c + 1, 0)
                 activate(c, r)
                 if r == 0 and c + 1 < N_CHUNKS:
-                    h_q[c + 1] = quantise_chunk(c + 1)
+                    quantise_chunk(c + 1)
                 if r == 1 and c > 0:
                     new_cell(c - 1)
                 if r == 2:

@@ -230,8 +230,13 @@ def tile_treelstmcell_kernel(
         def node_banks(c, name):
             return [(pair, slice(2 * pair, 2 * pair + 2), to_node_rows(gate[(c, name)], pair)) for pair in range(PAIRS)]
 
-        def dram_tiles(c, pair):
-            return slice(c * CHUNK_TILES + 2 * pair, c * CHUNK_TILES + 2 * pair + 2)
+        def pieces(c, pair):
+            widths = (1, 1) if (c == N_CHUNKS - 1 and pair == PAIRS - 1) else (2,)
+            found = []
+            for k, tiles in enumerate(widths):
+                first = 2 * pair + k
+                found.append((slice(k, k + tiles), slice(first, first + tiles), slice(c * CHUNK_TILES + first, c * CHUNK_TILES + first + tiles)))
+            return found
 
         def keep_child(c, child):
             kept = "kept%d" % child
@@ -243,34 +248,37 @@ def tile_treelstmcell_kernel(
                     out=node[(c, kept)][:, ts, :], in0=t_bank[:], in1=cm_sb[c][:, ts, child, :], op=ALU.mult
                 )
                 if child == 1:
-                    nc.gpsimd.tensor_tensor(
-                        out=node[(c, "c_red")][:, ts, :],
-                        in0=node[(c, "kept0")][:, ts, :],
-                        in1=node[(c, "kept1")][:, ts, :],
-                        op=ALU.add,
-                    )
+                    for in_bank, tiles, in_dram in pieces(c, pair):
+                        nc.gpsimd.tensor_tensor(
+                            out=node[(c, "c_red")][:, tiles, :],
+                            in0=node[(c, "kept0")][:, tiles, :],
+                            in1=node[(c, "kept1")][:, tiles, :],
+                            op=ALU.add,
+                        )
 
         def new_cell(c):
             new_node(c, "c")
             for pair, ts, t_bank in node_banks(c, "iu"):
-                nc.vector.tensor_tensor(
-                    out=node[(c, "c")][:, ts, :], in0=t_bank[:], in1=node[(c, "c_red")][:, ts, :], op=ALU.add
-                )
-                nc.sync.dma_start(out=c_out_view[:, dram_tiles(c, pair), :], in_=node[(c, "c")][:, ts, :])
+                for in_bank, tiles, in_dram in pieces(c, pair):
+                    nc.vector.tensor_tensor(
+                        out=node[(c, "c")][:, tiles, :], in0=t_bank[:, in_bank, :], in1=node[(c, "c_red")][:, tiles, :], op=ALU.add
+                    )
+                    nc.sync.dma_start(out=c_out_view[:, in_dram, :], in_=node[(c, "c")][:, tiles, :])
 
         def squash_cell(c):
             new_node(c, "tanh_c")
             for pair in range(PAIRS):
-                ts = slice(2 * pair, 2 * pair + 2)
-                nc.scalar.activation(out=node[(c, "tanh_c")][:, ts, :], in_=node[(c, "c")][:, ts, :], func=ACT.Tanh)
+                for in_bank, tiles, in_dram in pieces(c, pair):
+                    nc.scalar.activation(out=node[(c, "tanh_c")][:, tiles, :], in_=node[(c, "c")][:, tiles, :], func=ACT.Tanh)
 
         def new_hidden(c):
             new_node(c, "h")
             for pair, ts, t_bank in node_banks(c, "o"):
-                nc.vector.tensor_tensor(
-                    out=node[(c, "h")][:, ts, :], in0=t_bank[:], in1=node[(c, "tanh_c")][:, ts, :], op=ALU.mult
-                )
-                nc.sync.dma_start(out=h_out_view[:, dram_tiles(c, pair), :], in_=node[(c, "h")][:, ts, :])
+                for in_bank, tiles, in_dram in pieces(c, pair):
+                    nc.vector.tensor_tensor(
+                        out=node[(c, "h")][:, tiles, :], in0=t_bank[:, in_bank, :], in1=node[(c, "tanh_c")][:, tiles, :], op=ALU.mult
+                    )
+                    nc.sync.dma_start(out=h_out_view[:, in_dram, :], in_=node[(c, "h")][:, tiles, :])
 
         bias_rows_f32 = const.tile([P, P], F32, name="bias_rows_f32")
         bias_sb = const.tile([P, FEATURE_TILES], F32, name="bias_sb")

@@ -96,8 +96,9 @@ def tile_treelstmcell_kernel(
                 in_=dram[0].rearrange("p n t -> p (n t)")[:, 0 : cols * PACK].bitcast(I32),
             )
 
-        for pair in range(PAIRS):
-            load_h(0, 2 * pair, 2)
+        load_h(0, 0, 1)
+        load_h(0, 1, 1)
+        load_h(0, 2, 2)
         nc.scalar.dma_start(out=bias_rows[0:I_TILE, :], in_=U_f_b[0:D].rearrange("(m p) -> m p", p=P))
         nc.scalar.dma_start(out=bias_rows[I_TILE:FEATURE_TILES, :], in_=b_iou.rearrange("o (m p) -> (o m) p", p=P))
         load_codes(U_f_w_words, 0, D)
@@ -121,6 +122,17 @@ def tile_treelstmcell_kernel(
             h_codes = quant.tile([P, CHUNK], U32, name="h_codes", align_bytes=64)
             h_scales = quant.tile([P, CHUNK], U8, name="h_scales", align_bytes=64)
             h_q[c] = (h_codes, h_scales)
+
+        def transpose_tile(c, t):
+            h_bank = tp_psum.tile([P, 2, P], F32, name="h_bank", tag="tp")
+            words = h_sb[c][:, t, :].bitcast(F32)
+            for u in range(2):
+                nc.tensor.transpose(out=h_bank[:, u, :], in_=words[:, u : D // 2 : 2], identity=ident[:])
+            return h_bank
+
+        def group_tile(c, t, h_bank):
+            grouped_words = grouped[c][:].bitcast(F32).rearrange("p (n u) -> p n u", u=2)
+            nc.vector.tensor_copy(out=grouped_words[:, t * P : (t + 1) * P, :], in_=h_bank[:].rearrange("p u n -> p n u"))
 
         def transpose_h(c, pair):
             h_bank = tp_psum.tile([P, 2, 2 * P], F32, name="h_bank", tag="tp")
@@ -283,13 +295,15 @@ def tile_treelstmcell_kernel(
         bias_rows_f32 = const.tile([P, P], F32, name="bias_rows_f32")
         bias_sb = const.tile([P, FEATURE_TILES], F32, name="bias_sb")
         new_h_tiles(0)
-        h_banks = [transpose_h(0, pair) for pair in range(PAIRS)]
-        bias_bank = tp_psum.tile([P, 2, H], F32, name="bias_bank", tag="tp")
-        group_h(0, 0, h_banks[0])
+        tile_banks = [transpose_tile(0, t) for t in range(2)]
+        pair_bank = transpose_h(0, 1)
+        for t in range(2):
+            group_tile(0, t, tile_banks[t])
         nc.vector.tensor_copy(out=bias_rows_f32[:], in_=bias_rows[:])
+        bias_bank = tp_psum.tile([P, 2, H], F32, name="bias_bank", tag="tp")
         nc.tensor.transpose(out=bias_bank[:, 0, 0:P], in_=bias_rows_f32[:], identity=ident[:])
         quantise(0, 0, PAIR_NODES)
-        group_h(0, 1, h_banks[1])
+        group_h(0, 1, pair_bank)
         nc.vector.tensor_copy(out=bias_sb[:], in_=bias_bank[:, 0, 0:FEATURE_TILES])
         quantise(0, PAIR_NODES, PAIR_NODES)
 

@@ -253,20 +253,22 @@ def tile_treelstmcell_kernel(
         def keep_child(c, child):
             kept = "kept%d" % child
             new_node(c, kept)
-            if child == 1:
-                new_node(c, "c_red")
             for pair, ts, t_bank in node_banks(c, "f%d" % child):
                 nc.vector.tensor_tensor(
                     out=node[(c, kept)][:, ts, :], in0=t_bank[:], in1=cm_sb[c][:, ts, child, :], op=ALU.mult
                 )
-                if child == 1:
-                    for in_bank, tiles, in_dram in pieces(c, pair):
-                        nc.gpsimd.tensor_tensor(
-                            out=node[(c, "c_red")][:, tiles, :],
-                            in0=node[(c, "kept0")][:, tiles, :],
-                            in1=node[(c, "kept1")][:, tiles, :],
-                            op=ALU.add,
-                        )
+
+        def add_children(c, pairs):
+            if (c, "c_red") not in node:
+                new_node(c, "c_red")
+            for pair in pairs:
+                for in_bank, tiles, in_dram in pieces(c, pair):
+                    nc.gpsimd.tensor_tensor(
+                        out=node[(c, "c_red")][:, tiles, :],
+                        in0=node[(c, "kept0")][:, tiles, :],
+                        in1=node[(c, "kept1")][:, tiles, :],
+                        op=ALU.add,
+                    )
 
         def new_cell(c):
             new_node(c, "c")
@@ -307,26 +309,31 @@ def tile_treelstmcell_kernel(
         nc.vector.tensor_copy(out=bias_sb[:], in_=bias_bank[:, 0, 0:FEATURE_TILES])
         quantise(0, PAIR_NODES, PAIR_NODES)
 
-        multiply(0, 0)
+        BOTH = tuple(range(PAIRS))
+        LAST = N_CHUNKS - 1
+        sequence = [(c, r) for c in range(N_CHUNKS) for r in range(ROUNDS)]
+        after = {}
         for c in range(N_CHUNKS):
-            for r in range(ROUNDS):
-                if r + 1 < ROUNDS:
-                    multiply(c, r + 1)
-                elif c + 1 < N_CHUNKS:
-                    multiply(c + 1, 0)
-                activate(c, r)
-                if r == 0 and c + 1 < N_CHUNKS:
-                    quantise_chunk(c + 1)
-                if r == 1 and c > 0:
-                    new_cell(c - 1)
-                if r == 2:
-                    keep_child(c, 0)
-                if r == 3:
-                    keep_child(c, 1)
-                    if c > 0:
-                        squash_cell(c - 1)
-                if r == 4 and c > 0:
-                    new_hidden(c - 1)
-        new_cell(N_CHUNKS - 1)
-        squash_cell(N_CHUNKS - 1)
-        new_hidden(N_CHUNKS - 1)
+            after[(c, 0)] = [(quantise_chunk, c + 1)] if c < LAST else []
+            after[(c, 1)] = [(new_cell, c - 1)] if c > 0 else []
+            after[(c, 2)] = [(keep_child, c, 0)]
+            after[(c, 3)] = [(keep_child, c, 1), (add_children, c, BOTH)] + ([(squash_cell, c - 1)] if c > 0 else [])
+            after[(c, 4)] = [(new_hidden, c - 1)] if c > 0 else []
+        sequence.remove((LAST - 1, 4))
+        behind = sequence.index((LAST, 1)) + 1
+        sequence = sequence[:behind] + [(LAST - 1, 4)] + sequence[behind:]
+        after[(LAST - 1, 3)] = [(keep_child, LAST - 1, 1), (add_children, LAST - 1, BOTH)]
+        after[(LAST, 0)] = []
+        after[(LAST, 1)] = [(squash_cell, LAST - 2), (keep_child, LAST, 0)]
+        after[(LAST - 1, 4)] = [(keep_child, LAST, 1), (add_children, LAST, BOTH[:1]), (new_hidden, LAST - 2)]
+        after[(LAST, 2)] = [(new_cell, LAST - 1)]
+        after[(LAST, 3)] = [(add_children, LAST, BOTH[1:]), (squash_cell, LAST - 1)]
+        after[(LAST, 4)] = [(new_hidden, LAST - 1), (new_cell, LAST), (squash_cell, LAST), (new_hidden, LAST)]
+
+        multiply(*sequence[0])
+        for k in range(len(sequence)):
+            if k + 1 < len(sequence):
+                multiply(*sequence[k + 1])
+            activate(*sequence[k])
+            for stage in after[sequence[k]]:
+                stage[0](*stage[1:])

@@ -63,6 +63,9 @@ def tile_treelstmcell_kernel(
         ident = const.tile([P, P], F32, name="ident")
         make_identity(nc, ident[:])
 
+        one_column = const.tile([P, 2], F32, name="one_column")
+        nc.vector.memset(one_column[:, 0:1], 0.0)
+        nc.scalar.activation(out=one_column[:, 1:2], in_=one_column[:, 0:1], func=ACT.Sigmoid)
         bias_rows = const.tile([P, P], BF16, name="bias_rows")
         nc.vector.memset(bias_rows[:], 0.0)
         w_scales = const.tile([P, W_COLS], U8, name="w_scales", align_bytes=64)

@@ -323,14 +323,14 @@ def tile_treelstmcell_kernel(
             after[(c, 3)] = [(keep_child, c, 1), (add_children, c, BOTH)] + ([(squash_cell, c - 1)] if c > 0 else [])
             after[(c, 4)] = [(new_hidden, c - 1)] if c > 0 else []
         sequence.remove((LAST - 1, 4))
-        behind = sequence.index((LAST, 1)) + 1
+        behind = sequence.index((LAST, 3)) + 1
         sequence = sequence[:behind] + [(LAST - 1, 4)] + sequence[behind:]
         after[(LAST - 1, 3)] = [(keep_child, LAST - 1, 1), (add_children, LAST - 1, BOTH)]
-        after[(LAST, 0)] = []
-        after[(LAST, 1)] = [(squash_cell, LAST - 2), (keep_child, LAST, 0)]
-        after[(LAST - 1, 4)] = [(keep_child, LAST, 1), (add_children, LAST, BOTH[:1]), (new_hidden, LAST - 2)]
-        after[(LAST, 2)] = [(new_cell, LAST - 1)]
-        after[(LAST, 3)] = [(add_children, LAST, BOTH[1:]), (squash_cell, LAST - 1)]
+        after[(LAST, 0)] = [(squash_cell, LAST - 2), (new_hidden, LAST - 2)]
+        after[(LAST, 1)] = [(new_cell, LAST - 1)]
+        after[(LAST, 2)] = [(keep_child, LAST, 0)]
+        after[(LAST, 3)] = [(keep_child, LAST, 1), (add_children, LAST, BOTH)]
+        after[(LAST - 1, 4)] = [(squash_cell, LAST - 1)]
         after[(LAST, 4)] = [(new_hidden, LAST - 1), (new_cell, LAST), (squash_cell, LAST), (new_hidden, LAST)]
 
         multiply(*sequence[0])

@@ -197,12 +197,15 @@ def tile_treelstmcell_kernel(
                 return [(F_TILE + m, r * PAIR_NODES, PAIR_NODES, m // 2, (m % 2) * PAIR_NODES) for m in range(CHILDREN * HALVES)]
             return [(m, 0, CHUNK, j, 0) for j, m in enumerate(feature_tiles(r))]
 
-        def multiply(c, r):
+        def multiply(c, r, which=(0, 1)):
             h_codes, h_scales = h_q[c]
-            banks[(c, r)] = [mx_psum.tile([P, CHUNK], F32, name="bank", tag="mx") for j in range(2)]
+            for j in which:
+                banks[(c, r, j)] = mx_psum.tile([P, CHUNK], F32, name="bank", tag="mx")
             for m, first_node, nodes, j, first_col in passes(c, r):
+                if j not in which:
+                    continue
                 nc.tensor.matmul_mx(
-                    out=banks[(c, r)][j][:, first_col : first_col + nodes],
+                    out=banks[(c, r, j)][:, first_col : first_col + nodes],
                     lhsT=w_codes[:, m * P : (m + 1) * P].bitcast(FP8X4),
                     lhsT_scale=w_scales[:, m * P : (m + 1) * P],
                     rhs=h_codes[:, first_node : first_node + nodes].bitcast(FP8X4),
@@ -226,7 +229,7 @@ def tile_treelstmcell_kernel(
                     new_gate(c, name)
                 nc.scalar.activation(
                     out=gate[(c, name)][:, half, first_node : first_node + nodes],
-                    in_=banks[(c, r)][j][:, first_col : first_col + nodes],
+                    in_=banks[(c, r, j)][:, first_col : first_col + nodes],
                     func=ACT.Tanh if name == "u" else ACT.Sigmoid,
                     bias=bias_sb[:, m : m + 1],
                     scale=1.0,
@@ -242,8 +245,10 @@ def tile_treelstmcell_kernel(
         def new_node(c, name):
             node[(c, name)] = rows.tile([P, CHUNK_TILES, H], F32, name="node_" + name)
 
-        def node_banks(c, name):
-            return [(pair, slice(2 * pair, 2 * pair + 2), to_node_rows(gate[(c, name)], pair)) for pair in range(PAIRS)]
+        BOTH = tuple(range(PAIRS))
+
+        def node_banks(c, name, pairs=BOTH):
+            return [(pair, slice(2 * pair, 2 * pair + 2), to_node_rows(gate[(c, name)], pair)) for pair in pairs]
 
         def pieces(c, pair):
             widths = (1, 1) if (c == N_CHUNKS - 1 and pair == PAIRS - 1) else (2,)
@@ -253,10 +258,11 @@ def tile_treelstmcell_kernel(
                 found.append((slice(k, k + tiles), slice(first, first + tiles), slice(c * CHUNK_TILES + first, c * CHUNK_TILES + first + tiles)))
             return found
 
-        def keep_child(c, child):
+        def keep_child(c, child, pairs=BOTH):
             kept = "kept%d" % child
-            new_node(c, kept)
-            for pair, ts, t_bank in node_banks(c, "f%d" % child):
+            if (c, kept) not in node:
+                new_node(c, kept)
+            for pair, ts, t_bank in node_banks(c, "f%d" % child, pairs):
                 nc.vector.tensor_tensor(
                     out=node[(c, kept)][:, ts, :], in0=t_bank[:], in1=cm_sb[c][:, ts, child, :], op=ALU.mult
                 )
@@ -312,7 +318,6 @@ def tile_treelstmcell_kernel(
         nc.vector.tensor_copy(out=bias_sb[:], in_=bias_bank[:, 0, 0:FEATURE_TILES])
         quantise(0, PAIR_NODES, PAIR_NODES)
 
-        BOTH = tuple(range(PAIRS))
         LAST = N_CHUNKS - 1
         sequence = [(c, r) for c in range(N_CHUNKS) for r in range(ROUNDS)]
         after = {}
@@ -333,10 +338,28 @@ def tile_treelstmcell_kernel(
         after[(LAST - 1, 4)] = [(squash_cell, LAST - 1)]
         after[(LAST, 4)] = [(new_hidden, LAST - 1), (new_cell, LAST), (squash_cell, LAST), (new_hidden, LAST)]
 
-        multiply(*sequence[0])
+        split = [(c, 3) for c in range(1, N_CHUNKS)]
+        for c, r in split:
+            after[(c, 1)] = after[(c, 1)] + [(keep_child, c, 0, BOTH[:1])]
+            after[(c, 2)] = [(keep_child, c, 0, BOTH[1:])]
+
+        issued = set()
+
+        def issue(c, r, which=(0, 1)):
+            todo = tuple(j for j in which if (c, r, j) not in issued)
+            for j in todo:
+                issued.add((c, r, j))
+            multiply(c, r, todo)
+
+        issue(*sequence[0])
         for k in range(len(sequence)):
             if k + 1 < len(sequence):
-                multiply(*sequence[k + 1])
+                issue(*sequence[k + 1])
             activate(*sequence[k])
+            if k + 2 < len(sequence):
+                if sequence[k + 2] in split:
+                    issue(*sequence[k + 2], which=(0,))
+                if sequence[k + 1] in split:
+                    issue(*sequence[k + 2])
             for stage in after[sequence[k]]:
                 stage[0](*stage[1:])

from contextlib import ExitStack

import concourse.mybir as mybir
from concourse.masks import make_identity

F32 = mybir.dt.float32
BF16 = mybir.dt.bfloat16
I32 = mybir.dt.int32
U32 = mybir.dt.uint32
U8 = mybir.dt.uint8
FP8X4 = mybir.dt.float8_e4m3fn_x4
ACT = mybir.ActivationFunctionType
ALU = mybir.AluOpType

P = 128
PACK = 4
NODES = 2048
CHILDREN = 2
H = 256
D = CHILDREN * H
W_COLS = D + 3 * H
FEATURE_TILES = W_COLS // P
HALVES = H // P

NODE_TILES = NODES // P
CHUNK = 512
CHUNK_TILES = CHUNK // P
N_CHUNKS = NODES // CHUNK
PAIRS = CHUNK_TILES // 2

F_TILE = 0
I_TILE = D // P
O_TILE = I_TILE + HALVES
U_TILE = O_TILE + HALVES

FLOPS = 2 * NODES * D * W_COLS
BYTES = (
    2 * NODES * D * 2
    + D * W_COLS + (D // 32) * W_COLS + 2 * W_COLS
    + 2 * NODES * H * 4
)


def tile_treelstmcell_kernel(
    tc, h_mail, c_mail, U_f_w_words, U_f_w_scales, U_f_b, U_iou_w_words, U_iou_w_scales, b_iou, out_0, out_1
):
    nc = tc.nc
    h_view = h_mail.rearrange("(p t) k j -> p t (k j)", t=NODE_TILES)
    cm_view = c_mail.rearrange("(p t) k j -> p t k j", t=NODE_TILES)
    h_out_view = out_0.rearrange("(p t) j -> p t j", t=NODE_TILES)
    c_out_view = out_1.rearrange("(p t) j -> p t j", t=NODE_TILES)

    with ExitStack() as ctx:
        const = ctx.enter_context(tc.tile_pool(name="const", bufs=1))
        loads = ctx.enter_context(tc.tile_pool(name="loads", bufs=N_CHUNKS))
        quant = ctx.enter_context(tc.tile_pool(name="quant", bufs=2))
        gates = ctx.enter_context(tc.tile_pool(name="gates", bufs=2))
        rows = ctx.enter_context(tc.tile_pool(name="rows", bufs=3))
        mx_psum = ctx.enter_context(tc.psum_pool(name="mx_psum", bufs=4))
        tp_psum = ctx.enter_context(tc.psum_pool(name="tp_psum", bufs=4))
        ctx.enter_context(tc.manual_schedule())

        ident = const.tile([P, P], F32, name="ident")
        make_identity(nc, ident[:])

        one_column = const.tile([P, 2], F32, name="one_column")
        nc.vector.memset(one_column[:, 0:1], 0.0)
        nc.scalar.activation(out=one_column[:, 1:2], in_=one_column[:, 0:1], func=ACT.Sigmoid)
        bias_rows = const.tile([P, P], BF16, name="bias_rows")
        nc.vector.memset(bias_rows[:], 0.0)
        w_scales = const.tile([P, W_COLS], U8, name="w_scales", align_bytes=64)
        nc.vector.memset(w_scales[:].bitcast(I32), 0)
        w_codes = const.tile([P, W_COLS], U32, name="w_codes", align_bytes=64)

        h_sb = []
        cm_sb = []
        for c in range(N_CHUNKS):
            h_sb.append(loads.tile([P, CHUNK_TILES, D], BF16, name="h_sb", tag="h"))
            cm_sb.append(loads.tile([P, CHUNK_TILES, CHILDREN, H], BF16, name="cm_sb", tag="cm"))

        def load_h(c, first=0, tiles=CHUNK_TILES):
            nc.sync.dma_start(
                out=h_sb[c][:, first : first + tiles, :], in_=h_view[:, c * CHUNK_TILES + first : c * CHUNK_TILES + first + tiles, :]
            )

        def load_cm(c):
            nc.sync.dma_start(out=cm_sb[c][:], in_=cm_view[:, c * CHUNK_TILES : (c + 1) * CHUNK_TILES, :, :])

        def load_scales(dram, first_col, cols):
            for quad in range(4):
                nc.sync.dma_start(
                    out=w_scales[32 * quad : 32 * quad + 4, first_col : first_col + cols].bitcast(I32),
                    in_=dram[0, 4 * quad : 4 * quad + 4, 0:cols].bitcast(I32),
                )

        def load_codes(dram, first_col, cols):
            nc.sync.dma_start(
                out=w_codes[:, first_col : first_col + cols].bitcast(I32),
                in_=dram[0].rearrange("p n t -> p (n t)")[:, 0 : cols * PACK].bitcast(I32),
            )

        load_h(0, 0, 1)
        load_h(0, 1, 1)
        load_h(0, 2, 2)
        nc.scalar.dma_start(out=bias_rows[0:I_TILE, :], in_=U_f_b[0:D].rearrange("(m p) -> m p", p=P))
        nc.scalar.dma_start(out=bias_rows[I_TILE:FEATURE_TILES, :], in_=b_iou.rearrange("o (m p) -> (o m) p", p=P))
        load_codes(U_f_w_words, 0, D)
        load_scales(U_f_w_scales, 0, D)
        load_codes(U_iou_w_words, D, 3 * H)
        load_h(1)
        load_scales(U_iou_w_scales, D, 3 * H)
        load_cm(0)
        load_h(2)
        load_cm(1)
        load_h(3)
        load_cm(2)
        load_cm(3)

        grouped = {}
        h_q = {}
        PAIR_NODES = 2 * P

        def new_h_tiles(c):
            grouped[c] = quant.tile([P, CHUNK * PACK], BF16, name="grouped", align_bytes=64)
            h_codes = quant.tile([P, CHUNK], U32, name="h_codes", align_bytes=64)
            h_scales = quant.tile([P, CHUNK], U8, name="h_scales", align_bytes=64)
            h_q[c] = (h_codes, h_scales)

        def transpose_tile(c, t):
            h_bank = tp_psum.tile([P, 2, P], F32, name="h_bank", tag="tp")
            words = h_sb[c][:, t, :].bitcast(F32)
            for u in range(2):
                nc.tensor.transpose(out=h_bank[:, u, :], in_=words[:, u : D // 2 : 2], identity=ident[:])
            return h_bank

        def group_tile(c, t, h_bank):
            grouped_words = grouped[c][:].bitcast(F32).rearrange("p (n u) -> p n u", u=2)
            nc.vector.tensor_copy(out=grouped_words[:, t * P : (t + 1) * P, :], in_=h_bank[:].rearrange("p u n -> p n u"))

        def transpose_h(c, pair):
            h_bank = tp_psum.tile([P, 2, 2 * P], F32, name="h_bank", tag="tp")
            for tl in range(2):
                words = h_sb[c][:, 2 * pair + tl, :].bitcast(F32)
                for u in range(2):
                    nc.tensor.transpose(out=h_bank[:, u, tl * P : (tl + 1) * P], in_=words[:, u : D // 2 : 2], identity=ident[:])
            return h_bank

        def group_h(c, pair, h_bank):
            grouped_words = grouped[c][:].bitcast(F32).rearrange("p (n u) -> p n u", u=2)
            nc.vector.tensor_copy(
                out=grouped_words[:, pair * PAIR_NODES : (pair + 1) * PAIR_NODES, :], in_=h_bank[:].rearrange("p u n -> p n u")
            )

        def quantise(c, first_node, nodes):
            h_codes, h_scales = h_q[c]
            nc.vector.quantize_mx(
                out=h_codes[:, first_node : first_node + nodes].bitcast(FP8X4),
                scales=h_scales[:, first_node : first_node + nodes],
                in_=grouped[c][:, first_node * PACK : (first_node + nodes) * PACK],
            )

        def quantise_chunk(c):
            new_h_tiles(c)
            for pair in range(PAIRS):
                group_h(c, pair, transpose_h(c, pair))
            quantise(c, 0, CHUNK)

        def to_node_rows(src, pair):
            t_bank = tp_psum.tile([P, 2, H], F32, name="t_bank", tag="tp")
            for tl in range(2):
                t = 2 * pair + tl
                for half in range(HALVES):
                    nc.tensor.transpose(
                        out=t_bank[:, tl, half * P : (half + 1) * P],
                        in_=src[:, half, t * P : (t + 1) * P],
                        identity=ident[:],
                    )
            return t_bank

        ROUNDS = 5
        IU_ROUNDS = (2, 3)
        SIGMOID_ROUNDS = {0: ("f0", F_TILE), 1: ("f1", F_TILE + HALVES), 4: ("o", O_TILE)}
        banks = {}
        gate = {}
        node = {}

        def feature_tiles(r):
            if r in IU_ROUNDS:
                return (I_TILE + r - IU_ROUNDS[0], U_TILE + r - IU_ROUNDS[0])
            return (SIGMOID_ROUNDS[r][1], SIGMOID_ROUNDS[r][1] + 1)

        def by_pairs(c, r):
            return c == 0 and r < PAIRS

        def passes(c, r):
            if by_pairs(c, r):
                return [(F_TILE + m, r * PAIR_NODES, PAIR_NODES, m // 2, (m % 2) * PAIR_NODES) for m in range(CHILDREN * HALVES)]
            return [(m, 0, CHUNK, j, 0) for j, m in enumerate(feature_tiles(r))]

        def multiply(c, r, which=(0, 1)):
            h_codes, h_scales = h_q[c]
            for j in which:
                banks[(c, r, j)] = mx_psum.tile([P, CHUNK], F32, name="bank", tag="mx")
            for m, first_node, nodes, j, first_col in passes(c, r):
                if j not in which:
                    continue
                nc.tensor.matmul_mx(
                    out=banks[(c, r, j)][:, first_col : first_col + nodes],
                    lhsT=w_codes[:, m * P : (m + 1) * P].bitcast(FP8X4),
                    lhsT_scale=w_scales[:, m * P : (m + 1) * P],
                    rhs=h_codes[:, first_node : first_node + nodes].bitcast(FP8X4),
                    rhs_scale=h_scales[:, first_node : first_node + nodes],
                    start=True,
                    stop=True,
                )

        def new_gate(c, name):
            gate[(c, name)] = gates.tile([P, HALVES, CHUNK], F32, name="gate_" + name)

        GATE_OF_TILE = {}
        for name, first in (("f0", F_TILE), ("f1", F_TILE + HALVES), ("i", I_TILE), ("o", O_TILE), ("u", U_TILE)):
            for half in range(HALVES):
                GATE_OF_TILE[first + half] = (name, half)

        def activate(c, r):
            for m, first_node, nodes, j, first_col in passes(c, r):
                name, half = GATE_OF_TILE[m]
                if (c, name) not in gate:
                    new_gate(c, name)
                nc.scalar.activation(
                    out=gate[(c, name)][:, half, first_node : first_node + nodes],
                    in_=banks[(c, r, j)][:, first_col : first_col + nodes],
                    func=ACT.Tanh if name == "u" else ACT.Sigmoid,
                    bias=bias_sb[:, m : m + 1],
                    scale=1.0,
                )
            if r in IU_ROUNDS:
                half = r - IU_ROUNDS[0]
                if half == 0:
                    new_gate(c, "iu")
                nc.gpsimd.tensor_tensor(
                    out=gate[(c, "iu")][:, half, :], in0=gate[(c, "i")][:, half, :], in1=gate[(c, "u")][:, half, :], op=ALU.mult
                )

        def new_node(c, name):
            node[(c, name)] = rows.tile([P, CHUNK_TILES, H], F32, name="node_" + name)

        BOTH = tuple(range(PAIRS))

        def node_banks(c, name, pairs=BOTH):
            return [(pair, slice(2 * pair, 2 * pair + 2), to_node_rows(gate[(c, name)], pair)) for pair in pairs]

        def pieces(c, pair):
            widths = (1, 1) if (c == N_CHUNKS - 1 and pair == PAIRS - 1) else (2,)
            found = []
            for k, tiles in enumerate(widths):
                first = 2 * pair + k
                found.append((slice(k, k + tiles), slice(first, first + tiles), slice(c * CHUNK_TILES + first, c * CHUNK_TILES + first + tiles)))
            return found

        def keep_child(c, child, pairs=BOTH):
            kept = "kept%d" % child
            if (c, kept) not in node:
                new_node(c, kept)
            for pair, ts, t_bank in node_banks(c, "f%d" % child, pairs):
                nc.vector.tensor_tensor(
                    out=node[(c, kept)][:, ts, :], in0=t_bank[:], in1=cm_sb[c][:, ts, child, :], op=ALU.mult
                )

        def add_children(c, pairs):
            if (c, "c_red") not in node:
                new_node(c, "c_red")
            for pair in pairs:
                for in_bank, tiles, in_dram in pieces(c, pair):
                    nc.gpsimd.tensor_tensor(
                        out=node[(c, "c_red")][:, tiles, :],
                        in0=node[(c, "kept0")][:, tiles, :],
                        in1=node[(c, "kept1")][:, tiles, :],
                        op=ALU.add,
                    )

        def new_cell(c):
            new_node(c, "c")
            for pair, ts, t_bank in node_banks(c, "iu"):
                for in_bank, tiles, in_dram in pieces(c, pair):
                    nc.vector.tensor_tensor(
                        out=node[(c, "c")][:, tiles, :], in0=t_bank[:, in_bank, :], in1=node[(c, "c_red")][:, tiles, :], op=ALU.add
                    )
                    nc.sync.dma_start(out=c_out_view[:, in_dram, :], in_=node[(c, "c")][:, tiles, :])

        def squash_cell(c):
            new_node(c, "tanh_c")
            for pair in range(PAIRS):
                for in_bank, tiles, in_dram in pieces(c, pair):
                    nc.scalar.activation(out=node[(c, "tanh_c")][:, tiles, :], in_=node[(c, "c")][:, tiles, :], func=ACT.Tanh)

        def new_hidden(c):
            new_node(c, "h")
            for pair, ts, t_bank in node_banks(c, "o"):
                for in_bank, tiles, in_dram in pieces(c, pair):
                    nc.vector.tensor_tensor(
                        out=node[(c, "h")][:, tiles, :], in0=t_bank[:, in_bank, :], in1=node[(c, "tanh_c")][:, tiles, :], op=ALU.mult
                    )
                    nc.sync.dma_start(out=h_out_view[:, in_dram, :], in_=node[(c, "h")][:, tiles, :])

        bias_rows_f32 = const.tile([P, P], F32, name="bias_rows_f32")
        bias_sb = const.tile([P, FEATURE_TILES], F32, name="bias_sb")
        new_h_tiles(0)
        tile_banks = [transpose_tile(0, t) for t in range(2)]
        pair_bank = transpose_h(0, 1)
        for t in range(2):
            group_tile(0, t, tile_banks[t])
        nc.vector.tensor_copy(out=bias_rows_f32[:], in_=bias_rows[:])
        bias_bank = tp_psum.tile([P, 2, H], F32, name="bias_bank", tag="tp")
        nc.tensor.transpose(out=bias_bank[:, 0, 0:P], in_=bias_rows_f32[:], identity=ident[:])
        quantise(0, 0, PAIR_NODES)
        group_h(0, 1, pair_bank)
        nc.vector.tensor_copy(out=bias_sb[:], in_=bias_bank[:, 0, 0:FEATURE_TILES])
        quantise(0, PAIR_NODES, PAIR_NODES)

        LAST = N_CHUNKS - 1
        sequence = [(c, r) for c in range(N_CHUNKS) for r in range(ROUNDS)]
        after = {}
        for c in range(N_CHUNKS):
            after[(c, 0)] = [(quantise_chunk, c + 1)] if c < LAST else []
            after[(c, 1)] = [(new_cell, c - 1)] if c > 0 else []
            after[(c, 2)] = [(keep_child, c, 0)]
            after[(c, 3)] = [(keep_child, c, 1), (add_children, c, BOTH)] + ([(squash_cell, c - 1)] if c > 0 else [])
            after[(c, 4)] = [(new_hidden, c - 1)] if c > 0 else []
        sequence.remove((LAST - 1, 4))
        behind = sequence.index((LAST, 3)) + 1
        sequence = sequence[:behind] + [(LAST - 1, 4)] + sequence[behind:]
        after[(LAST - 1, 3)] = [(keep_child, LAST - 1, 1), (add_children, LAST - 1, BOTH)]
        after[(LAST, 0)] = [(squash_cell, LAST - 2), (new_hidden, LAST - 2)]
        after[(LAST, 1)] = [(new_cell, LAST - 1)]
        after[(LAST, 2)] = [(keep_child, LAST, 0)]
        after[(LAST, 3)] = [(keep_child, LAST, 1), (add_children, LAST, BOTH)]
        after[(LAST - 1, 4)] = [(squash_cell, LAST - 1)]
        after[(LAST, 4)] = [(new_hidden, LAST - 1), (new_cell, LAST), (squash_cell, LAST), (new_hidden, LAST)]

        split = [(c, 3) for c in range(1, N_CHUNKS)]
        for c, r in split:
            after[(c, 1)] = after[(c, 1)] + [(keep_child, c, 0, BOTH[:1])]
            after[(c, 2)] = [(keep_child, c, 0, BOTH[1:])]

        issued = set()

        def issue(c, r, which=(0, 1)):
            todo = tuple(j for j in which if (c, r, j) not in issued)
            for j in todo:
                issued.add((c, r, j))
            multiply(c, r, todo)

        issue(*sequence[0])
        for k in range(len(sequence)):
            if k + 1 < len(sequence):
                issue(*sequence[k + 1])
            activate(*sequence[k])
            if k + 2 < len(sequence):
                if sequence[k + 2] in split:
                    issue(*sequence[k + 2], which=(0,))
                if sequence[k + 1] in split:
                    issue(*sequence[k + 2])
            for stage in after[sequence[k]]:
                stage[0](*stage[1:])
